import numpy as np
import ml_dtypes


BF16 = ml_dtypes.bfloat16


def bf(x):
    return np.asarray(x, np.float32).astype(BF16)


def f64(x):
    return np.asarray(x).astype(np.float64)


E2M1 = np.array([0.0, 0.5, 1.0, 1.5, 2.0, 3.0, 4.0, 6.0, -0.0, -0.5, -1.0, -1.5, -2.0, -3.0, -4.0, -6.0])


def pack_weight(w, fmt):
    k, n = w.shape
    w = f64(bf(w)).reshape(k // 32, 32, n)
    amax = np.abs(w).max(1)
    if fmt == "e4m3":
        byte = np.frexp(amax)[1] - 1 + 127 - 7
    else:
        mant, ex = np.frexp(amax / 6.0)
        byte = np.where(mant > 0.5, ex, ex - 1) + 127
    byte = np.clip(np.where(amax > 0, byte, 1), 1, 254)
    scaled = (w * np.exp2(127.0 - byte)[:, None, :]).reshape(k, n).astype(np.float32)
    by_word = np.ascontiguousarray(scaled.reshape(k // 512, 128, 4, n).transpose(0, 1, 3, 2))
    if fmt == "e4m3":
        words = by_word.astype(ml_dtypes.float8_e4m3fn).view(np.uint8)
    else:
        c = by_word.astype(ml_dtypes.float4_e2m1fn).view(np.uint8) & 0xF
        words = c[..., 0::2] | (c[..., 1::2] << 4)
    return np.ascontiguousarray(words), np.ascontiguousarray(byte.astype(np.uint8).reshape(k // 512, 16, n))


def unpack_weight(words, scales, fmt):
    g, p, n, _ = words.shape
    if fmt == "e4m3":
        vals = np.ascontiguousarray(words).view(ml_dtypes.float8_e4m3fn).astype(np.float64)
    else:
        nib = np.empty((g, p, n, 4), np.uint8)
        nib[..., 0::2] = words & 0xF
        nib[..., 1::2] = words >> 4
        vals = E2M1[nib]
    vals = vals * np.repeat(np.exp2(scales.astype(np.float64) - 127.0), 8, axis=1)[..., None]
    return vals.transpose(0, 1, 3, 2).reshape(g * 512, n)

def pack4(w):
    words, scales = pack_weight(w, "e2m1")
    return words.reshape(words.shape[0], 128, -1), scales


def unpack4(words, scales):
    return unpack_weight(words.reshape(words.shape[0], 128, -1, 2), scales, "e2m1")


def kspread(k):
    return np.exp2(np.repeat(np.random.randint(-6, 7, k // 32), 32).astype(np.float64))


B, H, W, DIM, NH, HD, WH, WW = 8, 16, 16, 4096, 16, 64, 8, 8
E = NH * HD
N = WH * WW
HALF = HD // 2


def cos_sin(n):
    inv_freq = 1.0 / (10000.0 ** (f64(np.arange(0, HALF, 2)) / HALF))
    ang = f64(np.arange(n))[:, None] * inv_freq
    return np.concatenate([np.cos(ang)] * 2, -1), np.concatenate([np.sin(ang)] * 2, -1)


def rot_half(u):
    u1, u2 = np.split(u, 2, axis=-1)
    return np.concatenate([-u2, u1], -1)


def rope2(t):
    cos_h, sin_h = cos_sin(WH)
    cos_w, sin_w = cos_sin(WW)
    th, tw = t[..., :HALF], t[..., HALF:]
    th = th * cos_h[:, None, :] + rot_half(th) * sin_h[:, None, :]
    tw = tw * cos_w[None, :, :] + rot_half(tw) * sin_w[None, :, :]
    return np.concatenate([th, tw], -1)


def setup_inputs():
    s = kspread(DIM)
    x = np.random.standard_normal((B, H, W, DIM)) * s
    x_words, x_scales = pack4(np.ascontiguousarray(x.reshape(-1, DIM).T))
    qkv_w_words, qkv_w_scales = pack4(np.random.standard_normal((DIM, 3 * E)) / np.sqrt(DIM) / s[:, None])
    qkv_b = bf(np.random.standard_normal(3 * E) * 0.3)
    return {"x_words": x_words,
            "x_scales": x_scales,
            "qkv_w_words": qkv_w_words,
            "qkv_w_scales": qkv_w_scales,
            "qkv_b": qkv_b}


def reference(x_words, x_scales, qkv_w_words, qkv_w_scales, qkv_b):
    x = unpack4(x_words, x_scales).T.reshape(B, H, W, DIM)
    xw = x.reshape(B, H // WH, WH, W // WW, WW, DIM).transpose(0, 1, 3, 2, 4, 5).reshape(-1, N, DIM)
    BW = xw.shape[0]
    qkv = (xw @ unpack4(qkv_w_words, qkv_w_scales)) + f64(qkv_b)
    qkv = qkv.reshape(BW, N, 3, NH, HD).transpose(2, 0, 3, 1, 4)
    q, k, v = qkv[0], qkv[1], qkv[2]
    q = rope2(q.reshape(-1, WH, WW, HD)).reshape(BW, NH, N, HD)
    k = rope2(k.reshape(-1, WH, WW, HD)).reshape(BW, NH, N, HD)
    return q, k, np.ascontiguousarray(v)

@@ -1,0 +1,286 @@
+import math
+from contextlib import ExitStack
+
+import concourse.mybir as mybir
+
+FLOPS = 2 * 2048 * 4096 * 3072
+
+F32 = mybir.dt.float32
+BF16 = mybir.dt.bfloat16
+I32 = mybir.dt.int32
+U8 = mybir.dt.uint8
+FP4X4 = mybir.dt.float4_e2m1fn_x4
+ALU = mybir.AluOpType
+ACT = mybir.ActivationFunctionType
+
+P = 128
+PASSES = 8
+TILES = 16
+GROUP = 4
+E = 1024
+N = 512
+
+
+def tile_hydra_attn_pa_kernel(tc, x_words, x_scales, w_words, w_scales, b, q, k, v):
+    nc = tc.nc
+    outs = (q, k, v)
+
+    with ExitStack() as ctx:
+        keep = ctx.enter_context(tc.tile_pool(name="keep", bufs=1))
+        work = ctx.enter_context(tc.tile_pool(name="work", bufs=2))
+        stage = ctx.enter_context(tc.tile_pool(name="stage", bufs=6))
+        psum = ctx.enter_context(tc.psum_pool(name="psum", bufs=8))
+        ctx.enter_context(tc.manual_schedule())
+
+        xr = []
+        xsr = []
+        for i in range(2):
+            codes = keep.tile([P, PASSES, GROUP * 2 * P], U8, align_bytes=64, name="xr%d" % i)
+            plane = keep.tile([P, PASSES, GROUP * P], U8, align_bytes=64, name="xsr%d" % i)
+            xr.append(codes)
+            xsr.append(plane)
+        xc = []
+        xs = []
+        for i in range(4):
+            codes = keep.tile([P, PASSES, GROUP * 2 * P], U8, align_bytes=64, name="xc%d" % i)
+            plane = keep.tile([P, PASSES, GROUP * P], U8, align_bytes=64, name="xs%d" % i)
+            xc.append(codes)
+            xs.append(plane)
+        wc = []
+        ws = []
+        for i in range(3):
+            codes = keep.tile([P, PASSES, 2 * E], U8, align_bytes=64, name="wc%d" % i)
+            plane = keep.tile([P, PASSES, E], U8, align_bytes=64, name="ws%d" % i)
+            wc.append(codes)
+            ws.append(plane)
+        bias = keep.tile([P, 3 * E], F32, name="bias")
+        cos_t = keep.tile([P, 16, 2, 2, 16], F32, name="cos_t")
+        sin_t = keep.tile([P, 16, 2, 2, 16], F32, name="sin_t")
+        ones = keep.tile([P, P], BF16, name="ones")
+        brow_v = keep.tile([P, E], BF16, name="brow_v")
+        brow_qk = keep.tile([P, 2 * E], BF16, name="brow_qk")
+        pid = keep.tile([P, 1], I32, name="pid")
+        pos_i = keep.tile([P, 2], I32, name="pos_i")
+        pos = keep.tile([P, 2], F32, name="pos")
+        freq = keep.tile([P, 16], F32, name="freq")
+        arg = keep.tile([P, 2, 32], F32, name="arg")
+        wrap = keep.tile([P, 2, 32], F32, name="wrap")
+
+        def flat32(ap):
+            return ap.rearrange("p g b -> p (g b)").bitcast(I32)
+
+        def load_x(grp, g0, g1):
+            raw = xr[grp % 2]
+            c0 = grp * GROUP * 2 * P
+            nc.sync.dma_start(
+                out=raw[:, g0:g1, :].bitcast(I32),
+                in_=x_words[g0:g1, :, c0 : c0 + GROUP * 2 * P].rearrange("g p b -> p g b").bitcast(I32),
+            )
+
+        def load_w(part, g0, g1):
+            c0 = part * 2 * E
+            nc.sync.dma_start(
+                out=wc[part][:, g0:g1, :].bitcast(I32),
+                in_=w_words[g0:g1, :, c0 : c0 + 2 * E].rearrange("g p b -> p g b").bitcast(I32),
+            )
+
+        def load_scales(plane, scales, c0, c1, g0, g1):
+            for r in range(4):
+                nc.sync.dma_start(
+                    out=plane[r:P:32, g0:g1, :].bitcast(I32),
+                    in_=scales[g0:g1, r:16:4, c0:c1].rearrange("g q n -> q g n").bitcast(I32),
+                )
+
+        def zero(plane, g0, g1):
+            nc.vector.memset(flat32(plane[:, g0:g1, :]), 0)
+
+        def permute(dst, src, c):
+            nc.vector.tensor_copy(
+                out=dst.rearrange("p (x j r c) -> p x j r c", j=2, r=8, c=c),
+                in_=src.rearrange("p (x r j c) -> p x j r c", r=8, j=2, c=c),
+            )
+
+        load_x(0, 0, 1)
+        load_w(2, 0, 1)
+        nc.gpsimd.iota(pid[:], [[0, 1]], base=0, channel_multiplier=1)
+        nc.gpsimd.iota(freq[:], [[1, 16]], base=0, channel_multiplier=0, allow_small_or_imprecise_dtypes=True)
+        nc.gpsimd.memset(brow_v[:].bitcast(I32), 0)
+        nc.gpsimd.dma_start(out=brow_v[0:1, :], in_=b[2 * E : 3 * E].rearrange("(o n) -> o n", o=1))
+        nc.gpsimd.memset(ones[:], 1.0)
+        nc.gpsimd.memset(brow_qk[:].bitcast(I32), 0)
+        nc.gpsimd.dma_start(out=brow_qk[0:1, :], in_=b[0 : 2 * E].rearrange("(o n) -> o n", o=1))
+
+        zero(xsr[0], 0, 2)
+        zero(ws[2], 0, 2)
+        nc.vector.tensor_scalar(pos_i[:, 0:1], pid[:], 3, 7, op0=ALU.logical_shift_right, op1=ALU.bitwise_and)
+        nc.vector.tensor_scalar(pos_i[:, 1:2], pid[:], 7, None, op0=ALU.bitwise_and)
+        nc.vector.tensor_copy(out=pos[:], in_=pos_i[:])
+        nc.scalar.activation(freq[:], freq[:], ACT.Exp, scale=-math.log(10000.0) / 16)
+        for a in range(2):
+            nc.scalar.activation(arg[:, 0, 16 * a : 16 * a + 16], freq[:], ACT.Copy, scale=pos[:, a : a + 1])
+        nc.gpsimd.tensor_scalar(arg[:, 1, :], arg[:, 0, :], math.pi / 2, None, op0=ALU.add)
+        nc.gpsimd.tensor_scalar(wrap[:], arg[:], math.pi, -2 * math.pi, op0=ALU.is_ge, op1=ALU.mult)
+        nc.gpsimd.tensor_tensor(arg[:], arg[:], wrap[:], op=ALU.add)
+        load_scales(xsr[0], x_scales, 0, GROUP * P, 0, 2)
+        load_scales(ws[2], w_scales, 2 * E, 3 * E, 0, 2)
+        zero(xsr[0], 2, 8)
+        zero(ws[2], 2, 8)
+        load_x(0, 1, 2)
+        load_w(2, 1, 2)
+        load_scales(xsr[0], x_scales, 0, GROUP * P, 2, 8)
+        load_scales(ws[2], w_scales, 2 * E, 3 * E, 2, 8)
+        load_x(0, 2, 4)
+        load_w(2, 2, 3)
+        load_w(2, 3, 4)
+        load_x(0, 4, 8)
+        for g in range(4, 8):
+            load_w(2, g, g + 1)
+
+        for src, c0, n in ((brow_v, 2 * E, 2), (brow_qk, 0, 4)):
+            for i in range(n):
+                acc = psum.tile([P, N], F32, name="acc", tag="acc")
+                nc.tensor.matmul(acc[:], lhsT=ones[:], rhs=src[:, i * N : (i + 1) * N], start=True, stop=True)
+                nc.scalar.copy(out=bias[:, c0 + i * N : c0 + (i + 1) * N], in_=acc[:])
+
+        permute(flat32(xc[0][:, 0:1, :]), flat32(xr[0][:, 0:1, :]), 4)
+        permute(flat32(xs[0][:, 0:2, :]), flat32(xsr[0][:, 0:2, :]), 2)
+        permute(flat32(xc[0][:, 1:2, :]), flat32(xr[0][:, 1:2, :]), 4)
+        permute(flat32(xs[0][:, 2:8, :]), flat32(xsr[0][:, 2:8, :]), 2)
+        permute(flat32(xc[0][:, 2:4, :]), flat32(xr[0][:, 2:4, :]), 4)
+        permute(flat32(xc[0][:, 4:8, :]), flat32(xr[0][:, 4:8, :]), 4)
+        zero(ws[0], 0, 8)
+        zero(ws[1], 0, 8)
+        zero(xsr[1], 0, 8)
+
+        for half in range(2):
+            for table, which, sign in ((cos_t, 1, 1.0), (sin_t, 0, 2.0 * half - 1.0)):
+                nc.scalar.activation(
+                    table[:, :, :, half, :],
+                    arg[:, which, :].rearrange("p (a i) -> p a i", a=2).unsqueeze(1).to_broadcast([P, 16, 2, 16]),
+                    ACT.Sin,
+                    scale=sign,
+                )
+
+        def load_group(grp):
+            c0 = grp * GROUP * P
+            load_scales(xsr[grp % 2], x_scales, c0, c0 + GROUP * P, 0, 8)
+            load_x(grp, 0, 8)
+
+        for part in (0, 1):
+            load_scales(ws[part], w_scales, part * E, (part + 1) * E, 0, 8)
+            load_w(part, 0, 4)
+            load_w(part, 4, 8)
+        for grp in (1, 2):
+            load_group(grp)
+
+        def permute_group(grp):
+            permute(flat32(xc[grp][:]), flat32(xr[grp % 2][:]), 4)
+            permute(flat32(xs[grp][:]), flat32(xsr[grp % 2][:]), 2)
+
+        def mm(acc, t, part, c0, n, g):
+            grp, ti = divmod(t, GROUP)
+            nc.tensor.matmul_mx(
+                out=acc[:],
+                lhsT=xc[grp][:, g, ti * 2 * P : (ti + 1) * 2 * P].bitcast(FP4X4),
+                lhsT_scale=xs[grp][:, g, ti * P : (ti + 1) * P],
+                rhs=wc[part][:, g, 2 * c0 : 2 * (c0 + n)].bitcast(FP4X4),
+                rhs_scale=ws[part][:, g, c0 : c0 + n],
+                start=(g == 0),
+                stop=(g == PASSES - 1),
+            )
+
+        def add_bias(dst, acc, part, c0, n):
+            nc.vector.tensor_tensor(
+                dst[:, c0 : c0 + n], acc[:], bias[:, part * E + c0 : part * E + c0 + n], op=ALU.add
+            )
+
+        def store(src, t, part, c0, n):
+            h0, h1 = c0 // 64, (c0 + n) // 64
+            for j in range(2):
+                nc.scalar.dma_start(
+                    out=outs[part][2 * t + j, h0:h1].rearrange("h t d -> t h d"),
+                    in_=src[64 * j : 64 * j + 64, c0 : c0 + n].rearrange("p (h d) -> p h d", d=64),
+                )
+
+        def rope_halves(ap):
+            return ap.rearrange("p (x s i) -> p x s i", s=2, i=16)
+
+        pending = []
+
+        def finish_rope():
+            while pending:
+                t, part, o, m = pending.pop()
+                nc.vector.tensor_tensor(o[:], o[:], m[:], op=ALU.add)
+                store(o, t, part, 0, E)
+
+        def epilogue(t, part, accs):
+            if part == 2:
+                vo = stage.tile([P, E], F32, name="o", tag="o")
+                for acc, c0, n in accs:
+                    add_bias(vo, acc, part, c0, n)
+                finish_rope()
+                store(vo, t, part, 0, E)
+                return
+            y = work.tile([P, E], F32, name="y", tag="y")
+            for acc, c0, n in accs:
+                add_bias(y, acc, part, c0, n)
+            finish_rope()
+            o = stage.tile([P, E], F32, name="o", tag="o")
+            m = work.tile([P, E], F32, name="m", tag="m")
+            nc.vector.tensor_tensor(o[:], y[:], cos_t[:].rearrange("p h a s i -> p (h a s i)"), op=ALU.mult)
+            nc.vector.tensor_tensor(
+                rope_halves(m[:]),
+                rope_halves(y[:])[:, :, ::-1, :],
+                sin_t[:].rearrange("p h a s i -> p (h a) s i"),
+                op=ALU.mult,
+            )
+            pending.append((t, part, o, m))
+
+        def unit(t, part, widths):
+            accs = []
+            c0 = 0
+            for n in widths:
+                acc = psum.tile([P, n], F32, name="acc", tag="acc")
+                for g in range(PASSES):
+                    mm(acc, t, part, c0, n, g)
+                accs.append((acc, c0, n))
+                c0 += n
+            epilogue(t, part, accs)
+
+        sweep = []
+        for t in range(GROUP):
+            pair = []
+            for c0 in (0, N):
+                acc = psum.tile([P, N], F32, name="acc", tag="acc")
+                pair.append((acc, c0, N))
+            sweep.append(pair)
+        for g in range(PASSES):
+            for t in range(GROUP):
+                for acc, c0, n in sweep[t]:
+                    mm(acc, t, 2, c0, n, g)
+        for t in range(GROUP):
+            epilogue(t, 2, sweep[t])
+
+        for t in range(GROUP):
+            for part in (0, 1):
+                unit(t, part, (N, N))
+            if t < 3:
+                permute_group(t + 1)
+            if t == 0:
+                load_group(3)
+        for t in range(GROUP, TILES - 2):
+            for part in range(3):
+                unit(t, part, (N, N))
+        for t in range(TILES - 2, TILES):
+            for part in (0, 1):
+                unit(t, part, (N, N))
+        unit(TILES - 2, 2, (N, N))
+
+        t = TILES - 1
+        vo = stage.tile([P, E], F32, name="o", tag="o")
+        for c0, n in ((0, N), (N, N // 2), (N + N // 2, N // 2)):
+            acc = psum.tile([P, n], F32, name="acc", tag="acc")
+            for g in range(PASSES):
+                mm(acc, t, 2, c0, n, g)
+            add_bias(vo, acc, 2, c0, n)
+            store(vo, t, 2, c0, n)

@@ -19,6 +19,8 @@ TILES = 16
 GROUP = 4
 E = 1024
 N = 512
+BROWS = 8
+BCOLS = 3 * E // BROWS
 
 
 def tile_hydra_attn_pa_kernel(tc, x_words, x_scales, w_words, w_scales, b, q, k, v):
@@ -28,37 +30,37 @@ def tile_hydra_attn_pa_kernel(tc, x_words, x_scales, w_words, w_scales, b, q, k,
     with ExitStack() as ctx:
         keep = ctx.enter_context(tc.tile_pool(name="keep", bufs=1))
         work = ctx.enter_context(tc.tile_pool(name="work", bufs=2))
-        stage = ctx.enter_context(tc.tile_pool(name="stage", bufs=6))
+        stage = ctx.enter_context(tc.tile_pool(name="stage", bufs=5))
         psum = ctx.enter_context(tc.psum_pool(name="psum", bufs=8))
         ctx.enter_context(tc.manual_schedule())
 
         xr = []
         xsr = []
-        for i in range(2):
-            codes = keep.tile([P, PASSES, GROUP * 2 * P], U8, align_bytes=64, name="xr%d" % i)
-            plane = keep.tile([P, PASSES, GROUP * P], U8, align_bytes=64, name="xsr%d" % i)
+        for i in range(4):
+            codes = keep.tile([P, PASSES, GROUP * 2 * P], U8, align_bytes=256, name="xr%d" % i)
+            plane = keep.tile([P, PASSES, GROUP * P], U8, align_bytes=256, name="xsr%d" % i)
             xr.append(codes)
             xsr.append(plane)
         xc = []
         xs = []
         for i in range(4):
-            codes = keep.tile([P, PASSES, GROUP * 2 * P], U8, align_bytes=64, name="xc%d" % i)
-            plane = keep.tile([P, PASSES, GROUP * P], U8, align_bytes=64, name="xs%d" % i)
+            codes = keep.tile([P, PASSES, GROUP * 2 * P], U8, align_bytes=256, name="xc%d" % i)
+            plane = keep.tile([P, PASSES, GROUP * P], U8, align_bytes=256, name="xs%d" % i)
             xc.append(codes)
             xs.append(plane)
         wc = []
         ws = []
         for i in range(3):
-            codes = keep.tile([P, PASSES, 2 * E], U8, align_bytes=64, name="wc%d" % i)
-            plane = keep.tile([P, PASSES, E], U8, align_bytes=64, name="ws%d" % i)
+            codes = keep.tile([P, PASSES, 2 * E], U8, align_bytes=256, name="wc%d" % i)
+            plane = keep.tile([P, PASSES, E], U8, align_bytes=256, name="ws%d" % i)
             wc.append(codes)
             ws.append(plane)
         bias = keep.tile([P, 3 * E], F32, name="bias")
         cos_t = keep.tile([P, 16, 2, 2, 16], F32, name="cos_t")
         sin_t = keep.tile([P, 16, 2, 2, 16], F32, name="sin_t")
-        ones = keep.tile([P, P], BF16, name="ones")
-        brow_v = keep.tile([P, E], BF16, name="brow_v")
-        brow_qk = keep.tile([P, 2 * E], BF16, name="brow_qk")
+        brow = keep.tile([P, BCOLS], BF16, name="brow")
+        diff = keep.tile([P, BROWS], F32, name="diff")
+        pick = keep.tile([P, BROWS], BF16, name="pick")
         pid = keep.tile([P, 1], I32, name="pid")
         pos_i = keep.tile([P, 2], I32, name="pos_i")
         pos = keep.tile([P, 2], F32, name="pos")
@@ -70,7 +72,7 @@ def tile_hydra_attn_pa_kernel(tc, x_words, x_scales, w_words, w_scales, b, q, k,
             return ap.rearrange("p g b -> p (g b)").bitcast(I32)
 
         def load_x(grp, g0, g1):
-            raw = xr[grp % 2]
+            raw = xr[grp]
             c0 = grp * GROUP * 2 * P
             nc.sync.dma_start(
                 out=raw[:, g0:g1, :].bitcast(I32),
@@ -85,10 +87,10 @@ def tile_hydra_attn_pa_kernel(tc, x_words, x_scales, w_words, w_scales, b, q, k,
             )
 
         def load_scales(plane, scales, c0, c1, g0, g1):
-            for r in range(4):
+            for quad in range(4):
                 nc.sync.dma_start(
-                    out=plane[r:P:32, g0:g1, :].bitcast(I32),
-                    in_=scales[g0:g1, r:16:4, c0:c1].rearrange("g q n -> q g n").bitcast(I32),
+                    out=plane[32 * quad : 32 * quad + 4, g0:g1, :].bitcast(I32),
+                    in_=scales[g0:g1, 4 * quad : 4 * quad + 4, c0:c1].rearrange("g q n -> q g n").bitcast(I32),
                 )
 
         def zero(plane, g0, g1):
@@ -102,56 +104,72 @@ def tile_hydra_attn_pa_kernel(tc, x_words, x_scales, w_words, w_scales, b, q, k,
 
         load_x(0, 0, 1)
         load_w(2, 0, 1)
-        nc.gpsimd.iota(pid[:], [[0, 1]], base=0, channel_multiplier=1)
+        nc.gpsimd.memset(brow[:].bitcast(I32), 0)
+        nc.scalar.dma_start(out=brow[0:BROWS, :], in_=b.rearrange("(r n) -> r n", r=BROWS))
+        nc.gpsimd.iota(diff[:], [[-1, BROWS]], base=0, channel_multiplier=1, allow_small_or_imprecise_dtypes=True)
+        nc.gpsimd.tensor_scalar(pick[:], diff[:], 0.0, None, op0=ALU.is_equal)
         nc.gpsimd.iota(freq[:], [[1, 16]], base=0, channel_multiplier=0, allow_small_or_imprecise_dtypes=True)
-        nc.gpsimd.memset(brow_v[:].bitcast(I32), 0)
-        nc.gpsimd.dma_start(out=brow_v[0:1, :], in_=b[2 * E : 3 * E].rearrange("(o n) -> o n", o=1))
-        nc.gpsimd.memset(ones[:], 1.0)
-        nc.gpsimd.memset(brow_qk[:].bitcast(I32), 0)
-        nc.gpsimd.dma_start(out=brow_qk[0:1, :], in_=b[0 : 2 * E].rearrange("(o n) -> o n", o=1))
+        nc.gpsimd.iota(pid[:], [[0, 1]], base=0, channel_multiplier=1)
 
         zero(xsr[0], 0, 2)
-        zero(ws[2], 0, 2)
+        zero(ws[2], 0, 1)
+        zero(ws[2], 1, 3)
+        load_scales(xsr[0], x_scales, 0, GROUP * P, 0, 2)
+        load_scales(ws[2], w_scales, 2 * E, 3 * E, 0, 1)
+        nc.gpsimd.memset(flat32(xsr[0][:, 2:8, :]), 0)
+        zero(ws[2], 3, 8)
+        nc.scalar.activation(freq[:], freq[:], ACT.Exp, scale=-math.log(10000.0) / 16)
+        load_x(0, 1, 2)
+        load_w(2, 1, 2)
+        load_scales(ws[2], w_scales, 2 * E, 3 * E, 1, 3)
+        load_scales(xsr[0], x_scales, 0, GROUP * P, 2, 8)
+        load_w(2, 2, 3)
+        load_x(0, 2, 4)
+        load_w(2, 3, 4)
+        load_scales(ws[2], w_scales, 2 * E, 3 * E, 3, 5)
+        load_w(2, 4, 5)
+        load_x(0, 4, 8)
+        load_scales(ws[2], w_scales, 2 * E, 3 * E, 5, 8)
+        for g in range(5, 8):
+            load_w(2, g, g + 1)
+
+        spread = []
+        for i in range(BROWS // 2):
+            acc = psum.tile([P, 2 * BCOLS], BF16, name="acc", tag="acc")
+            for j in range(2):
+                r = 2 * i + j
+                nc.tensor.matmul(
+                    acc[:, j * BCOLS : (j + 1) * BCOLS],
+                    lhsT=pick[:, r : r + 1].to_broadcast([P, P]),
+                    rhs=brow[:],
+                    start=True,
+                    stop=True,
+                )
+            spread.append(acc)
+        def spread_bias(i, copy):
+            copy(out=bias[:, 2 * i * BCOLS : 2 * (i + 1) * BCOLS], in_=spread[i][:])
+
+        for i in (0, 2, 3):
+            spread_bias(i, nc.scalar.copy)
+
+        permute(flat32(xc[0][:, 0:1, :]), flat32(xr[0][:, 0:1, :]), 4)
+        permute(flat32(xs[0][:, 0:2, :]), flat32(xsr[0][:, 0:2, :]), 2)
+        spread_bias(1, nc.vector.tensor_copy)
+        permute(flat32(xc[0][:, 1:2, :]), flat32(xr[0][:, 1:2, :]), 4)
+        permute(flat32(xs[0][:, 2:8, :]), flat32(xsr[0][:, 2:8, :]), 2)
+        permute(flat32(xc[0][:, 2:4, :]), flat32(xr[0][:, 2:4, :]), 4)
+        permute(flat32(xc[0][:, 4:8, :]), flat32(xr[0][:, 4:8, :]), 4)
+        for plane in (xsr[1], ws[0], ws[1], xsr[2], xsr[3]):
+            zero(plane, 0, 8)
+
         nc.vector.tensor_scalar(pos_i[:, 0:1], pid[:], 3, 7, op0=ALU.logical_shift_right, op1=ALU.bitwise_and)
         nc.vector.tensor_scalar(pos_i[:, 1:2], pid[:], 7, None, op0=ALU.bitwise_and)
         nc.vector.tensor_copy(out=pos[:], in_=pos_i[:])
-        nc.scalar.activation(freq[:], freq[:], ACT.Exp, scale=-math.log(10000.0) / 16)
         for a in range(2):
             nc.scalar.activation(arg[:, 0, 16 * a : 16 * a + 16], freq[:], ACT.Copy, scale=pos[:, a : a + 1])
         nc.gpsimd.tensor_scalar(arg[:, 1, :], arg[:, 0, :], math.pi / 2, None, op0=ALU.add)
         nc.gpsimd.tensor_scalar(wrap[:], arg[:], math.pi, -2 * math.pi, op0=ALU.is_ge, op1=ALU.mult)
         nc.gpsimd.tensor_tensor(arg[:], arg[:], wrap[:], op=ALU.add)
-        load_scales(xsr[0], x_scales, 0, GROUP * P, 0, 2)
-        load_scales(ws[2], w_scales, 2 * E, 3 * E, 0, 2)
-        zero(xsr[0], 2, 8)
-        zero(ws[2], 2, 8)
-        load_x(0, 1, 2)
-        load_w(2, 1, 2)
-        load_scales(xsr[0], x_scales, 0, GROUP * P, 2, 8)
-        load_scales(ws[2], w_scales, 2 * E, 3 * E, 2, 8)
-        load_x(0, 2, 4)
-        load_w(2, 2, 3)
-        load_w(2, 3, 4)
-        load_x(0, 4, 8)
-        for g in range(4, 8):
-            load_w(2, g, g + 1)
-
-        for src, c0, n in ((brow_v, 2 * E, 2), (brow_qk, 0, 4)):
-            for i in range(n):
-                acc = psum.tile([P, N], F32, name="acc", tag="acc")
-                nc.tensor.matmul(acc[:], lhsT=ones[:], rhs=src[:, i * N : (i + 1) * N], start=True, stop=True)
-                nc.scalar.copy(out=bias[:, c0 + i * N : c0 + (i + 1) * N], in_=acc[:])
-
-        permute(flat32(xc[0][:, 0:1, :]), flat32(xr[0][:, 0:1, :]), 4)
-        permute(flat32(xs[0][:, 0:2, :]), flat32(xsr[0][:, 0:2, :]), 2)
-        permute(flat32(xc[0][:, 1:2, :]), flat32(xr[0][:, 1:2, :]), 4)
-        permute(flat32(xs[0][:, 2:8, :]), flat32(xsr[0][:, 2:8, :]), 2)
-        permute(flat32(xc[0][:, 2:4, :]), flat32(xr[0][:, 2:4, :]), 4)
-        permute(flat32(xc[0][:, 4:8, :]), flat32(xr[0][:, 4:8, :]), 4)
-        zero(ws[0], 0, 8)
-        zero(ws[1], 0, 8)
-        zero(xsr[1], 0, 8)
-
         for half in range(2):
             for table, which, sign in ((cos_t, 1, 1.0), (sin_t, 0, 2.0 * half - 1.0)):
                 nc.scalar.activation(
@@ -163,19 +181,21 @@ def tile_hydra_attn_pa_kernel(tc, x_words, x_scales, w_words, w_scales, b, q, k,
 
         def load_group(grp):
             c0 = grp * GROUP * P
-            load_scales(xsr[grp % 2], x_scales, c0, c0 + GROUP * P, 0, 8)
-            load_x(grp, 0, 8)
+            load_scales(xsr[grp], x_scales, c0, c0 + GROUP * P, 0, 8)
+            load_x(grp, 0, 4)
+            load_x(grp, 4, 8)
 
+        load_group(1)
         for part in (0, 1):
             load_scales(ws[part], w_scales, part * E, (part + 1) * E, 0, 8)
             load_w(part, 0, 4)
             load_w(part, 4, 8)
-        for grp in (1, 2):
-            load_group(grp)
+        load_group(2)
+        load_group(3)
 
         def permute_group(grp):
-            permute(flat32(xc[grp][:]), flat32(xr[grp % 2][:]), 4)
-            permute(flat32(xs[grp][:]), flat32(xsr[grp % 2][:]), 2)
+            permute(flat32(xc[grp][:]), flat32(xr[grp][:]), 4)
+            permute(flat32(xs[grp][:]), flat32(xsr[grp][:]), 2)
 
         def mm(acc, t, part, c0, n, g):
             grp, ti = divmod(t, GROUP)
@@ -258,17 +278,17 @@ def tile_hydra_attn_pa_kernel(tc, x_words, x_scales, w_words, w_scales, b, q, k,
             for t in range(GROUP):
                 for acc, c0, n in sweep[t]:
                     mm(acc, t, 2, c0, n, g)
+        permute_group(1)
         for t in range(GROUP):
             epilogue(t, 2, sweep[t])
-
-        for t in range(GROUP):
+        for t in range(GROUP, 2 * GROUP):
+            unit(t, 2, (N, N))
+        for t in range(2 * GROUP):
             for part in (0, 1):
                 unit(t, part, (N, N))
-            if t < 3:
-                permute_group(t + 1)
-            if t == 0:
-                load_group(3)
-        for t in range(GROUP, TILES - 2):
+            if t in (2, 5):
+                permute_group(2 if t == 2 else 3)
+        for t in range(2 * GROUP, TILES - 2):
             for part in range(3):
                 unit(t, part, (N, N))
         for t in range(TILES - 2, TILES):
@@ -278,7 +298,7 @@ def tile_hydra_attn_pa_kernel(tc, x_words, x_scales, w_words, w_scales, b, q, k,
 
         t = TILES - 1
         vo = stage.tile([P, E], F32, name="o", tag="o")
-        for c0, n in ((0, N), (N, N // 2), (N + N // 2, N // 2)):
+        for c0, n in ((0, 512), (512, 256), (768, 256)):
             acc = psum.tile([P, n], F32, name="acc", tag="acc")
             for g in range(PASSES):
                 mm(acc, t, 2, c0, n, g)

@@ -288,13 +288,14 @@ def tile_hydra_attn_pa_kernel(tc, x_words, x_scales, w_words, w_scales, b, q, k,
                 unit(t, part, (N, N))
             if t in (2, 5):
                 permute_group(2 if t == 2 else 3)
-        for t in range(2 * GROUP, TILES - 2):
+        for t in range(2 * GROUP, 3 * GROUP):
             for part in range(3):
                 unit(t, part, (N, N))
-        for t in range(TILES - 2, TILES):
+        for t in range(3 * GROUP, TILES):
             for part in (0, 1):
                 unit(t, part, (N, N))
-        unit(TILES - 2, 2, (N, N))
+        for t in range(3 * GROUP, TILES - 1):
+            unit(t, 2, (N, N))
 
         t = TILES - 1
         vo = stage.tile([P, E], F32, name="o", tag="o")

import math
from contextlib import ExitStack

import concourse.mybir as mybir

FLOPS = 2 * 2048 * 4096 * 3072

F32 = mybir.dt.float32
BF16 = mybir.dt.bfloat16
I32 = mybir.dt.int32
U8 = mybir.dt.uint8
FP4X4 = mybir.dt.float4_e2m1fn_x4
ALU = mybir.AluOpType
ACT = mybir.ActivationFunctionType

P = 128
PASSES = 8
TILES = 16
GROUP = 4
E = 1024
N = 512
BROWS = 8
BCOLS = 3 * E // BROWS


def tile_hydra_attn_pa_kernel(tc, x_words, x_scales, w_words, w_scales, b, q, k, v):
    nc = tc.nc
    outs = (q, k, v)

    with ExitStack() as ctx:
        keep = ctx.enter_context(tc.tile_pool(name="keep", bufs=1))
        work = ctx.enter_context(tc.tile_pool(name="work", bufs=2))
        stage = ctx.enter_context(tc.tile_pool(name="stage", bufs=5))
        psum = ctx.enter_context(tc.psum_pool(name="psum", bufs=8))
        ctx.enter_context(tc.manual_schedule())

        xr = []
        xsr = []
        for i in range(4):
            codes = keep.tile([P, PASSES, GROUP * 2 * P], U8, align_bytes=256, name="xr%d" % i)
            plane = keep.tile([P, PASSES, GROUP * P], U8, align_bytes=256, name="xsr%d" % i)
            xr.append(codes)
            xsr.append(plane)
        xc = []
        xs = []
        for i in range(4):
            codes = keep.tile([P, PASSES, GROUP * 2 * P], U8, align_bytes=256, name="xc%d" % i)
            plane = keep.tile([P, PASSES, GROUP * P], U8, align_bytes=256, name="xs%d" % i)
            xc.append(codes)
            xs.append(plane)
        wc = []
        ws = []
        for i in range(3):
            codes = keep.tile([P, PASSES, 2 * E], U8, align_bytes=256, name="wc%d" % i)
            plane = keep.tile([P, PASSES, E], U8, align_bytes=256, name="ws%d" % i)
            wc.append(codes)
            ws.append(plane)
        bias = keep.tile([P, 3 * E], F32, name="bias")
        cos_t = keep.tile([P, 16, 2, 2, 16], F32, name="cos_t")
        sin_t = keep.tile([P, 16, 2, 2, 16], F32, name="sin_t")
        brow = keep.tile([P, BCOLS], BF16, name="brow")
        diff = keep.tile([P, BROWS], F32, name="diff")
        pick = keep.tile([P, BROWS], BF16, name="pick")
        pid = keep.tile([P, 1], I32, name="pid")
        pos_i = keep.tile([P, 2], I32, name="pos_i")
        pos = keep.tile([P, 2], F32, name="pos")
        freq = keep.tile([P, 16], F32, name="freq")
        arg = keep.tile([P, 2, 32], F32, name="arg")
        wrap = keep.tile([P, 2, 32], F32, name="wrap")

        def flat32(ap):
            return ap.rearrange("p g b -> p (g b)").bitcast(I32)

        def load_x(grp, g0, g1):
            raw = xr[grp]
            c0 = grp * GROUP * 2 * P
            nc.sync.dma_start(
                out=raw[:, g0:g1, :].bitcast(I32),
                in_=x_words[g0:g1, :, c0 : c0 + GROUP * 2 * P].rearrange("g p b -> p g b").bitcast(I32),
            )

        def load_w(part, g0, g1):
            c0 = part * 2 * E
            nc.sync.dma_start(
                out=wc[part][:, g0:g1, :].bitcast(I32),
                in_=w_words[g0:g1, :, c0 : c0 + 2 * E].rearrange("g p b -> p g b").bitcast(I32),
            )

        def load_scales(plane, scales, c0, c1, g0, g1):
            for quad in range(4):
                nc.sync.dma_start(
                    out=plane[32 * quad : 32 * quad + 4, g0:g1, :].bitcast(I32),
                    in_=scales[g0:g1, 4 * quad : 4 * quad + 4, c0:c1].rearrange("g q n -> q g n").bitcast(I32),
                )

        def zero(plane, g0, g1):
            nc.vector.memset(flat32(plane[:, g0:g1, :]), 0)

        def permute(dst, src, c):
            nc.vector.tensor_copy(
                out=dst.rearrange("p (x j r c) -> p x j r c", j=2, r=8, c=c),
                in_=src.rearrange("p (x r j c) -> p x j r c", r=8, j=2, c=c),
            )

        load_x(0, 0, 1)
        load_w(2, 0, 1)
        nc.gpsimd.memset(brow[:].bitcast(I32), 0)
        nc.scalar.dma_start(out=brow[0:BROWS, :], in_=b.rearrange("(r n) -> r n", r=BROWS))
        nc.gpsimd.iota(diff[:], [[-1, BROWS]], base=0, channel_multiplier=1, allow_small_or_imprecise_dtypes=True)
        nc.gpsimd.tensor_scalar(pick[:], diff[:], 0.0, None, op0=ALU.is_equal)
        nc.gpsimd.iota(freq[:], [[1, 16]], base=0, channel_multiplier=0, allow_small_or_imprecise_dtypes=True)
        nc.gpsimd.iota(pid[:], [[0, 1]], base=0, channel_multiplier=1)

        zero(xsr[0], 0, 2)
        zero(ws[2], 0, 1)
        zero(ws[2], 1, 3)
        load_scales(xsr[0], x_scales, 0, GROUP * P, 0, 2)
        load_scales(ws[2], w_scales, 2 * E, 3 * E, 0, 1)
        nc.gpsimd.memset(flat32(xsr[0][:, 2:8, :]), 0)
        zero(ws[2], 3, 8)
        nc.scalar.activation(freq[:], freq[:], ACT.Exp, scale=-math.log(10000.0) / 16)
        load_x(0, 1, 2)
        load_w(2, 1, 2)
        load_scales(ws[2], w_scales, 2 * E, 3 * E, 1, 3)
        load_scales(xsr[0], x_scales, 0, GROUP * P, 2, 8)
        load_w(2, 2, 3)
        load_x(0, 2, 4)
        load_w(2, 3, 4)
        load_scales(ws[2], w_scales, 2 * E, 3 * E, 3, 5)
        load_w(2, 4, 5)
        load_x(0, 4, 8)
        load_scales(ws[2], w_scales, 2 * E, 3 * E, 5, 8)
        for g in range(5, 8):
            load_w(2, g, g + 1)

        spread = []
        for i in range(BROWS // 2):
            acc = psum.tile([P, 2 * BCOLS], BF16, name="acc", tag="acc")
            for j in range(2):
                r = 2 * i + j
                nc.tensor.matmul(
                    acc[:, j * BCOLS : (j + 1) * BCOLS],
                    lhsT=pick[:, r : r + 1].to_broadcast([P, P]),
                    rhs=brow[:],
                    start=True,
                    stop=True,
                )
            spread.append(acc)
        def spread_bias(i, copy):
            copy(out=bias[:, 2 * i * BCOLS : 2 * (i + 1) * BCOLS], in_=spread[i][:])

        for i in (0, 2, 3):
            spread_bias(i, nc.scalar.copy)

        permute(flat32(xc[0][:, 0:1, :]), flat32(xr[0][:, 0:1, :]), 4)
        permute(flat32(xs[0][:, 0:2, :]), flat32(xsr[0][:, 0:2, :]), 2)
        spread_bias(1, nc.vector.tensor_copy)
        permute(flat32(xc[0][:, 1:2, :]), flat32(xr[0][:, 1:2, :]), 4)
        permute(flat32(xs[0][:, 2:8, :]), flat32(xsr[0][:, 2:8, :]), 2)
        permute(flat32(xc[0][:, 2:4, :]), flat32(xr[0][:, 2:4, :]), 4)
        permute(flat32(xc[0][:, 4:8, :]), flat32(xr[0][:, 4:8, :]), 4)
        for plane in (xsr[1], ws[0], ws[1], xsr[2], xsr[3]):
            zero(plane, 0, 8)

        nc.vector.tensor_scalar(pos_i[:, 0:1], pid[:], 3, 7, op0=ALU.logical_shift_right, op1=ALU.bitwise_and)
        nc.vector.tensor_scalar(pos_i[:, 1:2], pid[:], 7, None, op0=ALU.bitwise_and)
        nc.vector.tensor_copy(out=pos[:], in_=pos_i[:])
        for a in range(2):
            nc.scalar.activation(arg[:, 0, 16 * a : 16 * a + 16], freq[:], ACT.Copy, scale=pos[:, a : a + 1])
        nc.gpsimd.tensor_scalar(arg[:, 1, :], arg[:, 0, :], math.pi / 2, None, op0=ALU.add)
        nc.gpsimd.tensor_scalar(wrap[:], arg[:], math.pi, -2 * math.pi, op0=ALU.is_ge, op1=ALU.mult)
        nc.gpsimd.tensor_tensor(arg[:], arg[:], wrap[:], op=ALU.add)
        for half in range(2):
            for table, which, sign in ((cos_t, 1, 1.0), (sin_t, 0, 2.0 * half - 1.0)):
                nc.scalar.activation(
                    table[:, :, :, half, :],
                    arg[:, which, :].rearrange("p (a i) -> p a i", a=2).unsqueeze(1).to_broadcast([P, 16, 2, 16]),
                    ACT.Sin,
                    scale=sign,
                )

        def load_group(grp):
            c0 = grp * GROUP * P
            load_scales(xsr[grp], x_scales, c0, c0 + GROUP * P, 0, 8)
            load_x(grp, 0, 4)
            load_x(grp, 4, 8)

        load_group(1)
        for part in (0, 1):
            load_scales(ws[part], w_scales, part * E, (part + 1) * E, 0, 8)
            load_w(part, 0, 4)
            load_w(part, 4, 8)
        load_group(2)
        load_group(3)

        def permute_group(grp):
            permute(flat32(xc[grp][:]), flat32(xr[grp][:]), 4)
            permute(flat32(xs[grp][:]), flat32(xsr[grp][:]), 2)

        def mm(acc, t, part, c0, n, g):
            grp, ti = divmod(t, GROUP)
            nc.tensor.matmul_mx(
                out=acc[:],
                lhsT=xc[grp][:, g, ti * 2 * P : (ti + 1) * 2 * P].bitcast(FP4X4),
                lhsT_scale=xs[grp][:, g, ti * P : (ti + 1) * P],
                rhs=wc[part][:, g, 2 * c0 : 2 * (c0 + n)].bitcast(FP4X4),
                rhs_scale=ws[part][:, g, c0 : c0 + n],
                start=(g == 0),
                stop=(g == PASSES - 1),
            )

        def add_bias(dst, acc, part, c0, n):
            nc.vector.tensor_tensor(
                dst[:, c0 : c0 + n], acc[:], bias[:, part * E + c0 : part * E + c0 + n], op=ALU.add
            )

        def store(src, t, part, c0, n):
            h0, h1 = c0 // 64, (c0 + n) // 64
            for j in range(2):
                nc.scalar.dma_start(
                    out=outs[part][2 * t + j, h0:h1].rearrange("h t d -> t h d"),
                    in_=src[64 * j : 64 * j + 64, c0 : c0 + n].rearrange("p (h d) -> p h d", d=64),
                )

        def rope_halves(ap):
            return ap.rearrange("p (x s i) -> p x s i", s=2, i=16)

        pending = []

        def finish_rope():
            while pending:
                t, part, o, m = pending.pop()
                nc.vector.tensor_tensor(o[:], o[:], m[:], op=ALU.add)
                store(o, t, part, 0, E)

        def epilogue(t, part, accs):
            if part == 2:
                vo = stage.tile([P, E], F32, name="o", tag="o")
                for acc, c0, n in accs:
                    add_bias(vo, acc, part, c0, n)
                finish_rope()
                store(vo, t, part, 0, E)
                return
            y = work.tile([P, E], F32, name="y", tag="y")
            for acc, c0, n in accs:
                add_bias(y, acc, part, c0, n)
            finish_rope()
            o = stage.tile([P, E], F32, name="o", tag="o")
            m = work.tile([P, E], F32, name="m", tag="m")
            nc.vector.tensor_tensor(o[:], y[:], cos_t[:].rearrange("p h a s i -> p (h a s i)"), op=ALU.mult)
            nc.vector.tensor_tensor(
                rope_halves(m[:]),
                rope_halves(y[:])[:, :, ::-1, :],
                sin_t[:].rearrange("p h a s i -> p (h a) s i"),
                op=ALU.mult,
            )
            pending.append((t, part, o, m))

        def unit(t, part, widths):
            accs = []
            c0 = 0
            for n in widths:
                acc = psum.tile([P, n], F32, name="acc", tag="acc")
                for g in range(PASSES):
                    mm(acc, t, part, c0, n, g)
                accs.append((acc, c0, n))
                c0 += n
            epilogue(t, part, accs)

        sweep = []
        for t in range(GROUP):
            pair = []
            for c0 in (0, N):
                acc = psum.tile([P, N], F32, name="acc", tag="acc")
                pair.append((acc, c0, N))
            sweep.append(pair)
        for g in range(PASSES):
            for t in range(GROUP):
                for acc, c0, n in sweep[t]:
                    mm(acc, t, 2, c0, n, g)
        permute_group(1)
        for t in range(GROUP):
            epilogue(t, 2, sweep[t])
        for t in range(GROUP, 2 * GROUP):
            unit(t, 2, (N, N))
        for t in range(2 * GROUP):
            for part in (0, 1):
                unit(t, part, (N, N))
            if t in (2, 5):
                permute_group(2 if t == 2 else 3)
        for t in range(2 * GROUP, 3 * GROUP):
            for part in range(3):
                unit(t, part, (N, N))
        for t in range(3 * GROUP, TILES):
            for part in (0, 1):
                unit(t, part, (N, N))
        for t in range(3 * GROUP, TILES - 1):
            unit(t, 2, (N, N))

        t = TILES - 1
        vo = stage.tile([P, E], F32, name="o", tag="o")
        for c0, n in ((0, 512), (512, 256), (768, 256)):
            acc = psum.tile([P, n], F32, name="acc", tag="acc")
            for g in range(PASSES):
                mm(acc, t, 2, c0, n, g)
            add_bias(vo, acc, 2, c0, n)
            store(vo, t, 2, c0, n)
